import numpy as np
import ml_dtypes


def mxq(x, axis, fmt="e4m3"):
    dtype, down = {"e4m3": (ml_dtypes.float8_e4m3fn, 7), "e5m2": (ml_dtypes.float8_e5m2, 14)}[fmt]
    v = np.moveaxis(np.asarray(x, np.float32).astype(ml_dtypes.bfloat16).astype(np.float64), axis, -1)
    blocks = v.reshape(v.shape[:-1] + (-1, 32))
    amax = np.abs(blocks).max(-1, keepdims=True)
    byte = np.maximum(np.where(amax > 0, np.frexp(amax)[1] - 1 + 127, 0) - down, 1)
    scale = np.exp2(byte - 127.0)
    codes = (blocks / scale).astype(np.float32).astype(dtype).astype(np.float64)
    return np.moveaxis((codes * scale).reshape(v.shape), -1, axis)


WIDE = False


def mx_kscale(k):
    if not WIDE:
        return np.ones(k)
    levels = np.array([10, -10, 5, -5, 0])
    a = np.random.permutation(np.resize(levels, k // 512 * 4)).reshape(k // 512, 4)
    idx = np.arange(k)
    return np.exp2(a[idx // 512, idx % 128 // 32])


BF16 = ml_dtypes.bfloat16


def bf(x):
    return np.asarray(x, np.float32).astype(BF16)


def f64(x):
    return np.asarray(x).astype(np.float64)


B, P, D, N = 4096, 1024, 1024, 1024
MINI, MAXI, EXPONENT = 0.001, 1.0, 4


def linear_normalization(maxi, mini, target_max, target_min):
    alpha = (target_max - target_min) / (maxi - mini)
    beta = target_min - alpha * mini
    return alpha, beta


def setup_inputs():
    s = mx_kscale(D)
    return {"x": bf(np.random.standard_normal((B, D)) * s),
            "x_dot": bf(np.random.standard_normal((B, D)) * 2.0 / np.sqrt(D)),
            "pos_sample": bf(np.random.standard_normal((P, D)) * s),
            "W": bf(np.random.standard_normal((D, N)) * 1.5 / np.sqrt(D * N) / s[:, None])}


def reference(x, x_dot, pos_sample, W):
    Wq = mxq(f64(W), 0, "e4m3")
    s_pos = mxq(f64(pos_sample), 1, "e4m3") @ Wq
    norm_pos = np.linalg.norm(s_pos, axis=1) ** EXPONENT
    alpha, beta = linear_normalization(norm_pos.max(), norm_pos.min(), MAXI, MINI)
    scores = mxq(f64(x), 1, "e4m3") @ Wq
    norm_power = np.linalg.norm(scores, axis=1) ** EXPONENT
    scale = alpha * norm_power + beta
    xd = f64(x_dot)
    return scale * np.sum(xd * xd, axis=1)

@@ -1,0 +1,359 @@
+from contextlib import ExitStack
+
+import concourse.mybir as mybir
+from concourse.masks import make_identity
+
+F32 = mybir.dt.float32
+BF16 = mybir.dt.bfloat16
+U32 = mybir.dt.uint32
+U8 = mybir.dt.uint8
+FP8X4 = mybir.dt.float8_e4m3fn_x4
+ACT = mybir.ActivationFunctionType
+ALU = mybir.AluOpType
+AX = mybir.AxisListType
+
+P = 128
+K = 1024
+N = 1024
+NH = 512
+B = 4096
+NPOS = 1024
+QUAD = 4
+POS_TILES = NPOS // P
+X_TILES = B // P
+TILES = POS_TILES + X_TILES
+CHUNKS = TILES // QUAD
+MINI = 0.001
+MAXI = 1.0
+
+FLOPS = 2 * (B + NPOS) * K * N
+
+XV_BEFORE = {2: 1, 3: 1, 4: 1, 5: 1, 6: 1, 7: 1, 8: 1, 9: 2}
+XV_AFTER = {2: 1, 3: 1, 4: 1, 5: 1, 6: 1, 7: 1, 8: 1, 9: 0}
+XS_AT = {2: (0,), 3: (0,), 4: (0,), 5: (0,), 6: (0,), 7: (0,), 8: (0,), 9: ()}
+XG_PERIODS = (2, 3, 4, 5, 6, 7)
+G_TILES = 7
+G_KEEP = 128
+G_EARLY = 4
+WARM_FIRST = 12
+RG_SPLIT = 336
+
+
+def tile_scoremagnitudemetric_kernel(tc, x, x_dot, pos_sample, W, out):
+    nc = tc.nc
+    with ExitStack() as ctx:
+        const = ctx.enter_context(tc.tile_pool(name="const", bufs=1))
+        rawp = ctx.enter_context(tc.tile_pool(name="rawp", bufs=4))
+        xdp = ctx.enter_context(tc.tile_pool(name="xdp", bufs=4))
+        grpp = ctx.enter_context(tc.tile_pool(name="grpp", bufs=3))
+        codep = ctx.enter_context(tc.tile_pool(name="codep", bufs=3))
+        gsqp = ctx.enter_context(tc.tile_pool(name="gsqp", bufs=2))
+        ps_t = ctx.enter_context(tc.psum_pool(name="ps_t", bufs=4))
+        ps_m = ctx.enter_context(tc.psum_pool(name="ps_m", bufs=4))
+        ctx.enter_context(tc.manual_schedule())
+
+        pos_v = pos_sample.rearrange("(p t) k -> p t k", t=POS_TILES)
+        x_v = x.rearrange("(p t) k -> p t k", t=X_TILES)
+        xd_v = x_dot.rearrange("(p t) k -> p t k", t=X_TILES)
+        out_v = out.rearrange("(p t) -> p t", t=X_TILES)
+
+        ident = const.tile([P, P], F32, name="ident")
+        w_raw = {}
+        for g in range(2):
+            for h in range(2):
+                w_piece = const.tile([P, 4, NH], BF16, name="w_piece", tag="w_raw%d%d" % (g, h))
+                w_raw[(g, h)] = w_piece
+        w_grp = const.tile([P, 2, N, 4], BF16, name="w_grp", align_bytes=64)
+        w_codes = const.tile([P, 2 * N], U32, name="w_codes", align_bytes=64)
+        w_scales = const.tile([P, 2 * N], U8, name="w_scales", align_bytes=64)
+        ssq = const.tile([P, TILES, 2], F32, name="ssq")
+        sd_s = const.tile([P, X_TILES], F32, name="sd_s")
+        sd_v = const.tile([P, X_TILES], F32, name="sd_v")
+        xst = const.tile([P, X_TILES, 2, 6], F32, name="xst")
+        xtmp = const.tile([P, 2, 4 * X_TILES], F32, name="xtmp")
+        gacc = const.tile([P, G_TILES, G_KEEP], F32, name="gacc")
+        warm = const.tile([P, 1], F32, name="warm")
+        zeros = const.tile([P, NH], BF16, name="zeros")
+        small = const.tile([P, 64], F32, name="small")
+        spread = const.tile([P, 2 * P], F32, name="spread")
+        fin = const.tile([P, 4, X_TILES], F32, name="fin")
+
+        raw = {}
+        xd = {}
+        grp = {}
+        codes = {}
+        scales = {}
+        tps = {}
+        state = {"xd_next": 0, "g_next": 0}
+
+        def load_w(g, h):
+            for u in range(2):
+                r0 = 512 * g + 256 * u
+                nc.sync.dma_start(
+                    out=w_raw[(g, h)][:, 2 * u : 2 * u + 2, :],
+                    in_=W[r0 : r0 + 256, h * NH : (h + 1) * NH].rearrange("(q e) c -> q e c", e=2),
+                )
+
+        def load_rows(c, a0, n):
+            if a0 == 0:
+                raw_t = rawp.tile([P, QUAD, K], BF16, name="raw_t", tag="raw")
+                raw[c] = raw_t
+            if c < 2:
+                src = pos_v[:, QUAD * c + a0 : QUAD * c + a0 + n, :]
+            else:
+                src = x_v[:, QUAD * (c - 2) + a0 : QUAD * (c - 2) + a0 + n, :]
+            nc.sync.dma_start(out=raw[c][:, a0 : a0 + n, :], in_=src)
+
+        def load_xd(d):
+            xd_t = xdp.tile([P, QUAD, K], BF16, name="xd_t", tag="xd")
+            xd[d] = xd_t
+            nc.sync.dma_start(out=xd_t[:], in_=xd_v[:, QUAD * d : QUAD * (d + 1), :])
+
+        def regroup_w(g, n0, n1, on_vector):
+            dst = w_grp[:, g, n0:n1, :].rearrange("p (c i) t -> p c t i", i=4)
+            h = n0 // NH
+            src = w_raw[(g, h)][:, :, n0 - h * NH : n1 - h * NH].rearrange("p t (c i) -> p c t i", i=4)
+            if on_vector:
+                nc.vector.tensor_copy(out=dst, in_=src)
+            else:
+                nc.scalar.copy(out=dst, in_=src)
+
+        def quantise_w(g, h):
+            cols = slice(g * N + h * NH, g * N + (h + 1) * NH)
+            nc.vector.quantize_mx(
+                out=w_codes[:, cols].bitcast(FP8X4),
+                scales=w_scales[:, cols],
+                in_=w_grp[:, g, h * NH : (h + 1) * NH, :].rearrange("p n t -> p (n t)"),
+            )
+
+        def transposes(j):
+            c, a = divmod(j, QUAD)
+            tp = ps_t.tile([P, 4, P], F32, name="tp", tag="tp")
+            tps[j] = tp
+            words = raw[c][:, a, :].bitcast(F32)
+            for q in range(4):
+                nc.tensor.transpose(tp[:, q, :], words[:, q * P : (q + 1) * P], ident[:])
+
+        def copy_out(j, on_vector):
+            c, a = divmod(j, QUAD)
+            if a == 0:
+                grp_t = grpp.tile([P, QUAD * K], BF16, name="grp_t", tag="grp", align_bytes=64)
+                grp[c] = grp_t
+            dst = grp[c][:, a * K : (a + 1) * K].bitcast(F32).rearrange("p (g r u) -> p g r u", g=2, u=2)
+            src = tps[j][:].rearrange("p (g u) r -> p g r u", g=2)
+            if on_vector:
+                nc.vector.tensor_copy(out=dst, in_=src)
+            else:
+                nc.scalar.copy(out=dst, in_=src)
+
+        def quantise(c, a0, n):
+            if a0 == 0:
+                codes_t = codep.tile([P, QUAD * 256], U32, name="codes_t", tag="codes", align_bytes=64)
+                scales_t = codep.tile([P, QUAD * 256], U8, name="scales_t", tag="scales", align_bytes=64)
+                codes[c] = codes_t
+                scales[c] = scales_t
+            nc.vector.quantize_mx(
+                out=codes[c][:, a0 * 256 : (a0 + n) * 256].bitcast(FP8X4),
+                scales=scales[c][:, a0 * 256 : (a0 + n) * 256],
+                in_=grp[c][:, a0 * K : (a0 + n) * K],
+            )
+
+        def scores(j, h):
+            c, a = divmod(j, QUAD)
+            acc = ps_m.tile([P, NH], F32, name="acc", tag="acc")
+            for g in range(2):
+                lcols = slice(a * 256 + g * P, a * 256 + (g + 1) * P)
+                rcols = slice(g * N + h * NH, g * N + (h + 1) * NH)
+                nc.tensor.matmul_mx(
+                    out=acc[:],
+                    lhsT=codes[c][:, lcols].bitcast(FP8X4),
+                    lhsT_scale=scales[c][:, lcols],
+                    rhs=w_codes[:, rcols].bitcast(FP8X4),
+                    rhs_scale=w_scales[:, rcols],
+                    start=(g == 0),
+                    stop=(g == 1),
+                )
+            nc.scalar.activation(
+                out=raw[c][:, a, h * NH : (h + 1) * NH], in_=acc[:], func=ACT.Square, accum_out=ssq[:, j, h : h + 1]
+            )
+
+        def xdot(engine, fence_chunk=None):
+            t = state["xd_next"]
+            state["xd_next"] = t + 1
+            d, a = divmod(t, QUAD)
+            rows = xd[d][:, a, :]
+            if engine == "V":
+                for i in range(2):
+                    nc.vector.bn_stats(out=xst[:, t, i, :], in_=rows[:, i * NH : (i + 1) * NH])
+            elif engine == "S":
+                nc.scalar.activation(out=rows, in_=rows, func=ACT.Square, accum_out=sd_s[:, t : t + 1])
+            else:
+                i = state["g_next"]
+                state["g_next"] = i + 1
+                nc.gpsimd.memset(grp[fence_chunk][:, 0:16], 0.0)
+                gsq = gsqp.tile([P, K], F32, name="gsq", tag="gsq")
+                nc.gpsimd.tensor_tensor(out=gsq[:], in0=rows, in1=rows, op=ALU.mult)
+                nc.gpsimd.tensor_tensor(out=gsq[:, 0:512], in0=gsq[:, 0:512], in1=gsq[:, 512:1024], op=ALU.add)
+                nc.gpsimd.tensor_tensor(out=gsq[:, 0:256], in0=gsq[:, 0:256], in1=gsq[:, 256:512], op=ALU.add)
+                nc.gpsimd.tensor_tensor(out=gacc[:, i, :], in0=gsq[:, 0:128], in1=gsq[:, 128:256], op=ALU.add)
+
+        def keep_clock(n):
+            idle = ps_m.tile([P, NH], F32, name="idle", tag="acc")
+            for i in range(n):
+                nc.tensor.matmul(out=idle[:], lhsT=zeros[:, 0:P], rhs=zeros[:], start=(i == 0), stop=(i == n - 1))
+
+        nc.vector.memset(zeros[:], 0.0)
+        make_identity(nc, ident[:])
+        nc.vector.memset(warm[:], 0.0)
+        nc.scalar.activation(out=warm[:], in_=warm[:], func=ACT.Square)
+        nc.vector.memset(sd_s[:], 0.0)
+        nc.vector.memset(xst[:], 0.0)
+
+        load_w(0, 0)
+        load_w(1, 0)
+        load_rows(0, 0, 2)
+        load_rows(0, 2, 2)
+        load_rows(1, 0, 2)
+        load_rows(1, 2, 2)
+        load_w(0, 1)
+        load_w(1, 1)
+        load_rows(2, 0, QUAD)
+        load_xd(0)
+        load_rows(3, 0, QUAD)
+        load_xd(1)
+
+        regroup_w(0, 0, NH, True)
+        regroup_w(1, RG_SPLIT, NH, False)
+        regroup_w(1, 0, RG_SPLIT, True)
+        quantise_w(0, 0)
+        quantise_w(1, 0)
+
+        keep_clock(WARM_FIRST)
+        transposes(0)
+        transposes(1)
+        keep_clock(1)
+        copy_out(0, False)
+        copy_out(1, True)
+        quantise(0, 0, 2)
+        transposes(2)
+        transposes(3)
+        keep_clock(2)
+        copy_out(2, False)
+        copy_out(3, True)
+        scores(0, 0)
+        scores(1, 0)
+        quantise(0, 2, 2)
+        for j in range(4, 8):
+            transposes(j)
+        copy_out(4, False)
+        copy_out(5, True)
+        quantise(1, 0, 2)
+        copy_out(6, False)
+        copy_out(7, True)
+        scores(2, 0)
+        scores(3, 0)
+        quantise(1, 2, 2)
+        regroup_w(0, NH, N, True)
+        regroup_w(1, NH + RG_SPLIT, N, False)
+        regroup_w(1, NH, NH + RG_SPLIT, True)
+        quantise_w(0, 1)
+        quantise_w(1, 1)
+        for j in range(4, 8):
+            scores(j, 0)
+        for a in range(QUAD):
+            transposes(8 + a)
+        for a in range(QUAD):
+            copy_out(8 + a, True)
+        for j in range(POS_TILES):
+            scores(j, 1)
+        quantise(2, 0, QUAD)
+        xdot("V")
+        xdot("G", 2)
+        xdot("S")
+
+        n_pos = small[:, 0:8]
+        loc_max = small[:, 16:17]
+        loc_min = small[:, 17:18]
+        g_max = small[:, 18:19]
+        g_min = small[:, 19:20]
+        g4_max = small[:, 24:25]
+        g4_min = small[:, 25:26]
+        span = small[:, 20:21]
+        alpha = small[:, 21:22]
+        beta = small[:, 22:23]
+        for p in range(2, CHUNKS):
+            if p + 2 < CHUNKS:
+                load_rows(p + 2, 0, QUAD)
+            if p < X_TILES // QUAD:
+                load_xd(p)
+            if p == 5:
+                stat = ps_t.tile([P, 4, P], F32, name="stat", tag="tp")
+                nc.tensor.transpose(stat[:, 0, :], spread[:, 0:P], ident[:])
+                nc.tensor.transpose(stat[:, 1, :], spread[:, P : 2 * P], ident[:])
+                nc.vector.tensor_reduce(out=g_max, in_=stat[:, 0, :], axis=AX.X, op=ALU.max)
+                nc.vector.tensor_reduce(out=g_min, in_=stat[:, 1, :], axis=AX.X, op=ALU.min)
+            if p + 1 < CHUNKS:
+                for a in range(QUAD):
+                    transposes(QUAD * (p + 1) + a)
+                for a in range(QUAD):
+                    copy_out(QUAD * (p + 1) + a, True)
+            for i in range(XV_BEFORE[p]):
+                xdot("V")
+            if p + 1 < CHUNKS:
+                quantise(p + 1, 0, QUAD)
+            for i in range(XV_AFTER[p]):
+                xdot("V")
+            if p in XG_PERIODS:
+                xdot("G", p + 1)
+            if p == 3:
+                nc.vector.tensor_reduce(out=n_pos, in_=ssq[:, 0:POS_TILES, :], axis=AX.X, op=ALU.add)
+                nc.vector.tensor_reduce(out=loc_max, in_=n_pos, axis=AX.X, op=ALU.max)
+                nc.vector.tensor_reduce(out=loc_min, in_=n_pos, axis=AX.X, op=ALU.min)
+            if p == 8:
+                nc.vector.tensor_tensor(out=small[:, 24:26], in0=small[:, 18:20], in1=small[:, 18:20], op=ALU.mult)
+                nc.vector.tensor_tensor(out=span, in0=g4_max, in1=g4_min, op=ALU.subtract)
+                nc.vector.reciprocal(out=span, in_=span)
+                nc.vector.tensor_scalar(out=alpha, in0=span, scalar1=MAXI - MINI, scalar2=None, op0=ALU.mult)
+                nc.vector.tensor_tensor(out=beta, in0=alpha, in1=g4_min, op=ALU.mult)
+                nc.vector.tensor_scalar(out=beta, in0=beta, scalar1=-1.0, scalar2=MINI, op0=ALU.mult, op1=ALU.add)
+            if p == 6 or p == 9:
+                g0, g1 = (0, G_EARLY) if p == 6 else (G_EARLY, G_TILES)
+                nc.vector.tensor_reduce(
+                    out=xst[:].rearrange("p (d a) i v -> p d a i v", a=QUAD)[:, g0:g1, 1, 0, 2],
+                    in_=gacc[:, g0:g1, :],
+                    axis=AX.X,
+                    op=ALU.add,
+                )
+            if p == 9:
+                trip = xst[:].rearrange("p t i (e v) -> p (t i e) v", v=3)
+                nc.vector.tensor_tensor(out=xtmp[:, 0, :], in0=trip[:, :, 1], in1=trip[:, :, 1], op=ALU.mult)
+                nc.vector.scalar_tensor_tensor(
+                    out=xtmp[:, 1, :], in0=xtmp[:, 0, :], scalar=float(NH // 2), in1=trip[:, :, 2], op0=ALU.mult, op1=ALU.add
+                )
+                nc.vector.tensor_reduce(
+                    out=sd_v[:], in_=xtmp[:, 1, :].rearrange("p (t f) -> p t f", f=4), axis=AX.X, op=ALU.add
+                )
+                nc.vector.tensor_tensor(out=fin[:, 0, :], in0=sd_s[:], in1=sd_v[:], op=ALU.add)
+            k = 0
+            for h in range(2):
+                for a in range(QUAD):
+                    if k in XS_AT[p]:
+                        xdot("S")
+                    if p == 4 and k == 4:
+                        nc.scalar.copy(
+                            out=spread[:].rearrange("p (w c) -> p w c", w=2),
+                            in_=small[:, 16:18].unsqueeze(2).to_broadcast([P, 2, P]),
+                        )
+                    scores(QUAD * p + a, h)
+                    k += 1
+
+        nc.vector.tensor_tensor(
+            out=fin[:, 1, :], in0=ssq[:, POS_TILES:TILES, 0], in1=ssq[:, POS_TILES:TILES, 1], op=ALU.add
+        )
+        nc.vector.scalar_tensor_tensor(
+            out=fin[:, 2, :], in0=fin[:, 1, :], scalar=alpha, in1=fin[:, 1, :], op0=ALU.mult, op1=ALU.mult
+        )
+        nc.vector.scalar_tensor_tensor(
+            out=fin[:, 3, :], in0=fin[:, 2, :], scalar=beta, in1=fin[:, 0, :], op0=ALU.add, op1=ALU.mult
+        )
+        nc.sync.dma_start(out=out_v, in_=fin[:, 3, :])

@@ -28,13 +28,15 @@ MAXI = 1.0
 
 FLOPS = 2 * (B + NPOS) * K * N
 
-XV_BEFORE = {2: 1, 3: 1, 4: 1, 5: 1, 6: 1, 7: 1, 8: 1, 9: 2}
-XV_AFTER = {2: 1, 3: 1, 4: 1, 5: 1, 6: 1, 7: 1, 8: 1, 9: 0}
-XS_AT = {2: (0,), 3: (0,), 4: (0,), 5: (0,), 6: (0,), 7: (0,), 8: (0,), 9: ()}
-XG_PERIODS = (2, 3, 4, 5, 6, 7)
-G_TILES = 7
+S_COPIES = (0, 3, 5)
+XV = {0: 1, 1: 5, 2: 6, 3: 6, 4: 5}
+XG = {0: 2, 1: 2, 2: 2, 3: 3, 4: 0}
+OCT = 8
+GROUPS = X_TILES // OCT
+G_LIST = (1, 5, 9, 13, 17, 21, 25, 29, 31)
+G_TILES = len(G_LIST)
+RG_PIECE = 128
 G_KEEP = 128
-G_EARLY = 4
 WARM_FIRST = 12
 RG_SPLIT = 336
 
@@ -43,10 +45,11 @@ def tile_scoremagnitudemetric_kernel(tc, x, x_dot, pos_sample, W, out):
     nc = tc.nc
     with ExitStack() as ctx:
         const = ctx.enter_context(tc.tile_pool(name="const", bufs=1))
-        rawp = ctx.enter_context(tc.tile_pool(name="rawp", bufs=4))
-        xdp = ctx.enter_context(tc.tile_pool(name="xdp", bufs=4))
-        grpp = ctx.enter_context(tc.tile_pool(name="grpp", bufs=3))
-        codep = ctx.enter_context(tc.tile_pool(name="codep", bufs=3))
+        rawp = ctx.enter_context(tc.tile_pool(name="rawp", bufs=6))
+        xdp = ctx.enter_context(tc.tile_pool(name="xdp", bufs=5))
+        grpp = ctx.enter_context(tc.tile_pool(name="grpp", bufs=5))
+        codep = ctx.enter_context(tc.tile_pool(name="codep", bufs=5))
+        junkp = ctx.enter_context(tc.tile_pool(name="junkp", bufs=4))
         gsqp = ctx.enter_context(tc.tile_pool(name="gsqp", bufs=2))
         ps_t = ctx.enter_context(tc.psum_pool(name="ps_t", bufs=4))
         ps_m = ctx.enter_context(tc.psum_pool(name="ps_m", bufs=4))
@@ -67,15 +70,12 @@ def tile_scoremagnitudemetric_kernel(tc, x, x_dot, pos_sample, W, out):
         w_codes = const.tile([P, 2 * N], U32, name="w_codes", align_bytes=64)
         w_scales = const.tile([P, 2 * N], U8, name="w_scales", align_bytes=64)
         ssq = const.tile([P, TILES, 2], F32, name="ssq")
-        sd_s = const.tile([P, X_TILES], F32, name="sd_s")
-        sd_v = const.tile([P, X_TILES], F32, name="sd_v")
         xst = const.tile([P, X_TILES, 2, 6], F32, name="xst")
         xtmp = const.tile([P, 2, 4 * X_TILES], F32, name="xtmp")
         gacc = const.tile([P, G_TILES, G_KEEP], F32, name="gacc")
         warm = const.tile([P, 1], F32, name="warm")
         zeros = const.tile([P, NH], BF16, name="zeros")
         small = const.tile([P, 64], F32, name="small")
-        spread = const.tile([P, 2 * P], F32, name="spread")
         fin = const.tile([P, 4, X_TILES], F32, name="fin")
 
         raw = {}
@@ -85,6 +85,7 @@ def tile_scoremagnitudemetric_kernel(tc, x, x_dot, pos_sample, W, out):
         scales = {}
         tps = {}
         state = {"xd_next": 0, "g_next": 0}
+        rest = [t for t in range(X_TILES) if t not in G_LIST]
 
         def load_w(g, h):
             for u in range(2):
@@ -113,10 +114,12 @@ def tile_scoremagnitudemetric_kernel(tc, x, x_dot, pos_sample, W, out):
             dst = w_grp[:, g, n0:n1, :].rearrange("p (c i) t -> p c t i", i=4)
             h = n0 // NH
             src = w_raw[(g, h)][:, :, n0 - h * NH : n1 - h * NH].rearrange("p t (c i) -> p c t i", i=4)
-            if on_vector:
+            if on_vector == "V":
                 nc.vector.tensor_copy(out=dst, in_=src)
-            else:
+            elif on_vector == "S":
                 nc.scalar.copy(out=dst, in_=src)
+            else:
+                nc.gpsimd.tensor_scalar(out=dst, in0=src, scalar1=1.0, scalar2=0.0, op0=ALU.mult, op1=ALU.add)
 
         def quantise_w(g, h):
             cols = slice(g * N + h * NH, g * N + (h + 1) * NH)
@@ -173,24 +176,25 @@ def tile_scoremagnitudemetric_kernel(tc, x, x_dot, pos_sample, W, out):
                     start=(g == 0),
                     stop=(g == 1),
                 )
-            nc.scalar.activation(
-                out=raw[c][:, a, h * NH : (h + 1) * NH], in_=acc[:], func=ACT.Square, accum_out=ssq[:, j, h : h + 1]
-            )
+            junk = junkp.tile([P, NH], BF16, name="junk", tag="junk")
+            nc.scalar.activation(out=junk[:], in_=acc[:], func=ACT.Square, accum_out=ssq[:, j, h : h + 1])
 
         def xdot(engine, fence_chunk=None):
-            t = state["xd_next"]
-            state["xd_next"] = t + 1
+            if engine == "G":
+                t = G_LIST[state["g_next"]]
+            else:
+                t = rest[state["xd_next"]]
+                state["xd_next"] += 1
             d, a = divmod(t, QUAD)
             rows = xd[d][:, a, :]
             if engine == "V":
                 for i in range(2):
                     nc.vector.bn_stats(out=xst[:, t, i, :], in_=rows[:, i * NH : (i + 1) * NH])
-            elif engine == "S":
-                nc.scalar.activation(out=rows, in_=rows, func=ACT.Square, accum_out=sd_s[:, t : t + 1])
             else:
                 i = state["g_next"]
                 state["g_next"] = i + 1
-                nc.gpsimd.memset(grp[fence_chunk][:, 0:16], 0.0)
+                if fence_chunk is not None:
+                    nc.gpsimd.memset(grp[fence_chunk][:, 0:16], 0.0)
                 gsq = gsqp.tile([P, K], F32, name="gsq", tag="gsq")
                 nc.gpsimd.tensor_tensor(out=gsq[:], in0=rows, in1=rows, op=ALU.mult)
                 nc.gpsimd.tensor_tensor(out=gsq[:, 0:512], in0=gsq[:, 0:512], in1=gsq[:, 512:1024], op=ALU.add)
@@ -206,26 +210,30 @@ def tile_scoremagnitudemetric_kernel(tc, x, x_dot, pos_sample, W, out):
         make_identity(nc, ident[:])
         nc.vector.memset(warm[:], 0.0)
         nc.scalar.activation(out=warm[:], in_=warm[:], func=ACT.Square)
-        nc.vector.memset(sd_s[:], 0.0)
         nc.vector.memset(xst[:], 0.0)
 
         load_w(0, 0)
         load_w(1, 0)
-        load_rows(0, 0, 2)
+        load_rows(0, 0, 1)
+        load_rows(0, 1, 1)
         load_rows(0, 2, 2)
-        load_rows(1, 0, 2)
-        load_rows(1, 2, 2)
         load_w(0, 1)
+        load_rows(1, 0, 2)
         load_w(1, 1)
-        load_rows(2, 0, QUAD)
-        load_xd(0)
-        load_rows(3, 0, QUAD)
-        load_xd(1)
+        load_rows(1, 2, 2)
+        for kind, i in (
+            ("x", 2), ("x", 3), ("d", 0), ("x", 4), ("x", 5), ("d", 1), ("d", 2),
+        ):
+            if kind == "x":
+                load_rows(i, 0, QUAD)
+            else:
+                load_xd(i)
 
-        regroup_w(0, 0, NH, True)
-        regroup_w(1, RG_SPLIT, NH, False)
-        regroup_w(1, 0, RG_SPLIT, True)
+        regroup_w(0, RG_SPLIT, NH, "S")
+        regroup_w(0, 0, RG_SPLIT, "V")
         quantise_w(0, 0)
+        regroup_w(1, RG_SPLIT, NH, "S")
+        regroup_w(1, 0, RG_SPLIT, "V")
         quantise_w(1, 0)
 
         keep_clock(WARM_FIRST)
@@ -233,43 +241,41 @@ def tile_scoremagnitudemetric_kernel(tc, x, x_dot, pos_sample, W, out):
         transposes(1)
         keep_clock(1)
         copy_out(0, False)
-        copy_out(1, True)
-        quantise(0, 0, 2)
+        quantise(0, 0, 1)
+        copy_out(1, False)
+        quantise(0, 1, 1)
         transposes(2)
         transposes(3)
-        keep_clock(2)
-        copy_out(2, False)
-        copy_out(3, True)
+        copy_out(2, True)
+        copy_out(3, False)
         scores(0, 0)
         scores(1, 0)
         quantise(0, 2, 2)
-        for j in range(4, 8):
-            transposes(j)
-        copy_out(4, False)
+        transposes(4)
+        transposes(5)
+        copy_out(4, True)
         copy_out(5, True)
-        quantise(1, 0, 2)
-        copy_out(6, False)
-        copy_out(7, True)
         scores(2, 0)
         scores(3, 0)
+        quantise(1, 0, 2)
+        transposes(6)
+        transposes(7)
+        copy_out(6, True)
+        copy_out(7, False)
+        scores(4, 0)
+        scores(5, 0)
         quantise(1, 2, 2)
-        regroup_w(0, NH, N, True)
-        regroup_w(1, NH + RG_SPLIT, N, False)
-        regroup_w(1, NH, NH + RG_SPLIT, True)
-        quantise_w(0, 1)
-        quantise_w(1, 1)
-        for j in range(4, 8):
-            scores(j, 0)
-        for a in range(QUAD):
-            transposes(8 + a)
-        for a in range(QUAD):
-            copy_out(8 + a, True)
-        for j in range(POS_TILES):
-            scores(j, 1)
-        quantise(2, 0, QUAD)
-        xdot("V")
-        xdot("G", 2)
-        xdot("S")
+        for g in range(2):
+            for n0 in range(NH, N, RG_PIECE):
+                regroup_w(g, n0, n0 + RG_PIECE, "G")
+            quantise_w(g, 1)
+        scores(6, 0)
+        scores(7, 0)
+        def transpose_group(g):
+            for i in range(OCT):
+                transposes(OCT * g + i)
+            for i in range(OCT):
+                copy_out(OCT * g + i, i not in S_COPIES)
 
         n_pos = small[:, 0:8]
         loc_max = small[:, 16:17]
@@ -281,71 +287,73 @@ def tile_scoremagnitudemetric_kernel(tc, x, x_dot, pos_sample, W, out):
         span = small[:, 20:21]
         alpha = small[:, 21:22]
         beta = small[:, 22:23]
-        for p in range(2, CHUNKS):
-            if p + 2 < CHUNKS:
-                load_rows(p + 2, 0, QUAD)
-            if p < X_TILES // QUAD:
-                load_xd(p)
-            if p == 5:
+
+        load_rows(6, 0, QUAD)
+        load_rows(7, 0, QUAD)
+        load_xd(3)
+        load_xd(4)
+        transpose_group(1)
+        load_rows(8, 0, QUAD)
+        load_rows(9, 0, QUAD)
+        for j in range(POS_TILES):
+            scores(j, 1)
+        quantise(2, 0, QUAD)
+        quantise(3, 0, QUAD)
+        for i in range(XG[0]):
+            xdot("G", None)
+        for i in range(XV[0]):
+            xdot("V")
+
+        for p in range(1, GROUPS + 1):
+            if p < GROUPS:
+                transpose_group(p + 1)
+                quantise(2 * p + 2, 0, QUAD)
+                quantise(2 * p + 3, 0, QUAD)
+            else:
                 stat = ps_t.tile([P, 4, P], F32, name="stat", tag="tp")
-                nc.tensor.transpose(stat[:, 0, :], spread[:, 0:P], ident[:])
-                nc.tensor.transpose(stat[:, 1, :], spread[:, P : 2 * P], ident[:])
+                nc.tensor.transpose(stat[:, 0, :], loc_max.to_broadcast([P, P]), ident[:])
+                nc.tensor.transpose(stat[:, 1, :], loc_min.to_broadcast([P, P]), ident[:])
                 nc.vector.tensor_reduce(out=g_max, in_=stat[:, 0, :], axis=AX.X, op=ALU.max)
                 nc.vector.tensor_reduce(out=g_min, in_=stat[:, 1, :], axis=AX.X, op=ALU.min)
-            if p + 1 < CHUNKS:
-                for a in range(QUAD):
-                    transposes(QUAD * (p + 1) + a)
-                for a in range(QUAD):
-                    copy_out(QUAD * (p + 1) + a, True)
-            for i in range(XV_BEFORE[p]):
-                xdot("V")
-            if p + 1 < CHUNKS:
-                quantise(p + 1, 0, QUAD)
-            for i in range(XV_AFTER[p]):
-                xdot("V")
-            if p in XG_PERIODS:
-                xdot("G", p + 1)
-            if p == 3:
-                nc.vector.tensor_reduce(out=n_pos, in_=ssq[:, 0:POS_TILES, :], axis=AX.X, op=ALU.add)
-                nc.vector.tensor_reduce(out=loc_max, in_=n_pos, axis=AX.X, op=ALU.max)
-                nc.vector.tensor_reduce(out=loc_min, in_=n_pos, axis=AX.X, op=ALU.min)
-            if p == 8:
                 nc.vector.tensor_tensor(out=small[:, 24:26], in0=small[:, 18:20], in1=small[:, 18:20], op=ALU.mult)
                 nc.vector.tensor_tensor(out=span, in0=g4_max, in1=g4_min, op=ALU.subtract)
                 nc.vector.reciprocal(out=span, in_=span)
                 nc.vector.tensor_scalar(out=alpha, in0=span, scalar1=MAXI - MINI, scalar2=None, op0=ALU.mult)
                 nc.vector.tensor_tensor(out=beta, in0=alpha, in1=g4_min, op=ALU.mult)
                 nc.vector.tensor_scalar(out=beta, in0=beta, scalar1=-1.0, scalar2=MINI, op0=ALU.mult, op1=ALU.add)
-            if p == 6 or p == 9:
-                g0, g1 = (0, G_EARLY) if p == 6 else (G_EARLY, G_TILES)
+            for i in range(XG[p]):
+                xdot("G", None)
+            for i in range(XV[p]):
+                xdot("V")
+            if p == 1:
+                load_xd(5)
+            if p == 2:
+                load_xd(6)
+                load_xd(7)
+            if p == 1:
+                nc.vector.tensor_reduce(out=n_pos, in_=ssq[:, 0:POS_TILES, :], axis=AX.X, op=ALU.add)
+                nc.vector.tensor_reduce(out=loc_max, in_=n_pos, axis=AX.X, op=ALU.max)
+                nc.vector.tensor_reduce(out=loc_min, in_=n_pos, axis=AX.X, op=ALU.min)
+            if p == 3:
                 nc.vector.tensor_reduce(
-                    out=xst[:].rearrange("p (d a) i v -> p d a i v", a=QUAD)[:, g0:g1, 1, 0, 2],
-                    in_=gacc[:, g0:g1, :],
-                    axis=AX.X,
-                    op=ALU.add,
+                    out=xst[:].rearrange("p (d a) i v -> p d a i v", a=QUAD)[:, 0:5, 1, 0, 2], in_=gacc[:, 0:5, :], axis=AX.X, op=ALU.add
                 )
-            if p == 9:
+            if p == GROUPS:
+                nc.vector.tensor_reduce(
+                    out=xst[:].rearrange("p (d a) i v -> p d a i v", a=QUAD)[:, 5:8, 1, 0, 2], in_=gacc[:, 5:8, :], axis=AX.X, op=ALU.add
+                )
+                nc.vector.tensor_reduce(out=xst[:, 31, 0, 2:3], in_=gacc[:, 8:9, :], axis=AX.X, op=ALU.add)
                 trip = xst[:].rearrange("p t i (e v) -> p (t i e) v", v=3)
                 nc.vector.tensor_tensor(out=xtmp[:, 0, :], in0=trip[:, :, 1], in1=trip[:, :, 1], op=ALU.mult)
                 nc.vector.scalar_tensor_tensor(
                     out=xtmp[:, 1, :], in0=xtmp[:, 0, :], scalar=float(NH // 2), in1=trip[:, :, 2], op0=ALU.mult, op1=ALU.add
                 )
                 nc.vector.tensor_reduce(
-                    out=sd_v[:], in_=xtmp[:, 1, :].rearrange("p (t f) -> p t f", f=4), axis=AX.X, op=ALU.add
+                    out=fin[:, 0, :], in_=xtmp[:, 1, :].rearrange("p (t f) -> p t f", f=4), axis=AX.X, op=ALU.add
                 )
-                nc.vector.tensor_tensor(out=fin[:, 0, :], in0=sd_s[:], in1=sd_v[:], op=ALU.add)
-            k = 0
-            for h in range(2):
-                for a in range(QUAD):
-                    if k in XS_AT[p]:
-                        xdot("S")
-                    if p == 4 and k == 4:
-                        nc.scalar.copy(
-                            out=spread[:].rearrange("p (w c) -> p w c", w=2),
-                            in_=small[:, 16:18].unsqueeze(2).to_broadcast([P, 2, P]),
-                        )
-                    scores(QUAD * p + a, h)
-                    k += 1
+            for i in range(OCT):
+                for h in range(2):
+                    scores(OCT * p + i, h)
 
         nc.vector.tensor_tensor(
             out=fin[:, 1, :], in0=ssq[:, POS_TILES:TILES, 0], in1=ssq[:, POS_TILES:TILES, 1], op=ALU.add

@@ -29,15 +29,12 @@ MAXI = 1.0
 FLOPS = 2 * (B + NPOS) * K * N
 
 S_COPIES = (0, 3, 5)
-XV = {0: 1, 1: 5, 2: 6, 3: 6, 4: 5}
-XG = {0: 2, 1: 2, 2: 2, 3: 3, 4: 0}
 OCT = 8
-GROUPS = X_TILES // OCT
-G_LIST = (1, 5, 9, 13, 17, 21, 25, 29, 31)
+G_LIST = (1, 3, 5, 7, 9, 11, 13, 17, 21, 25, 29)
 G_TILES = len(G_LIST)
-RG_PIECE = 128
-G_KEEP = 128
-WARM_FIRST = 12
+RG_G = 320
+G_KEEP = 256
+WARM_FIRST = 10
 RG_SPLIT = 336
 
 
@@ -46,13 +43,12 @@ def tile_scoremagnitudemetric_kernel(tc, x, x_dot, pos_sample, W, out):
     with ExitStack() as ctx:
         const = ctx.enter_context(tc.tile_pool(name="const", bufs=1))
         rawp = ctx.enter_context(tc.tile_pool(name="rawp", bufs=6))
-        xdp = ctx.enter_context(tc.tile_pool(name="xdp", bufs=5))
-        grpp = ctx.enter_context(tc.tile_pool(name="grpp", bufs=5))
+        xdp = ctx.enter_context(tc.tile_pool(name="xdp", bufs=6))
+        grpp = ctx.enter_context(tc.tile_pool(name="grpp", bufs=4))
         codep = ctx.enter_context(tc.tile_pool(name="codep", bufs=5))
         junkp = ctx.enter_context(tc.tile_pool(name="junkp", bufs=4))
-        gsqp = ctx.enter_context(tc.tile_pool(name="gsqp", bufs=2))
-        ps_t = ctx.enter_context(tc.psum_pool(name="ps_t", bufs=4))
-        ps_m = ctx.enter_context(tc.psum_pool(name="ps_m", bufs=4))
+        gsqp = ctx.enter_context(tc.tile_pool(name="gsqp", bufs=3))
+        ps = ctx.enter_context(tc.psum_pool(name="ps", bufs=8))
         ctx.enter_context(tc.manual_schedule())
 
         pos_v = pos_sample.rearrange("(p t) k -> p t k", t=POS_TILES)
@@ -84,7 +80,7 @@ def tile_scoremagnitudemetric_kernel(tc, x, x_dot, pos_sample, W, out):
         codes = {}
         scales = {}
         tps = {}
-        state = {"xd_next": 0, "g_next": 0}
+        state = {"xd_next": 0}
         rest = [t for t in range(X_TILES) if t not in G_LIST]
 
         def load_w(g, h):
@@ -131,7 +127,7 @@ def tile_scoremagnitudemetric_kernel(tc, x, x_dot, pos_sample, W, out):
 
         def transposes(j):
             c, a = divmod(j, QUAD)
-            tp = ps_t.tile([P, 4, P], F32, name="tp", tag="tp")
+            tp = ps.tile([P, 4, P], F32, name="tp", tag="bank")
             tps[j] = tp
             words = raw[c][:, a, :].bitcast(F32)
             for q in range(4):
@@ -163,7 +159,7 @@ def tile_scoremagnitudemetric_kernel(tc, x, x_dot, pos_sample, W, out):
 
         def scores(j, h):
             c, a = divmod(j, QUAD)
-            acc = ps_m.tile([P, NH], F32, name="acc", tag="acc")
+            acc = ps.tile([P, NH], F32, name="acc", tag="bank")
             for g in range(2):
                 lcols = slice(a * 256 + g * P, a * 256 + (g + 1) * P)
                 rcols = slice(g * N + h * NH, g * N + (h + 1) * NH)
@@ -179,30 +175,38 @@ def tile_scoremagnitudemetric_kernel(tc, x, x_dot, pos_sample, W, out):
             junk = junkp.tile([P, NH], BF16, name="junk", tag="junk")
             nc.scalar.activation(out=junk[:], in_=acc[:], func=ACT.Square, accum_out=ssq[:, j, h : h + 1])
 
-        def xdot(engine, fence_chunk=None):
-            if engine == "G":
-                t = G_LIST[state["g_next"]]
-            else:
+        def xd_rows(t):
+            d, a = divmod(t, QUAD)
+            return xd[d][:, a, :]
+
+        def squares_v(n):
+            for i in range(n):
                 t = rest[state["xd_next"]]
                 state["xd_next"] += 1
-            d, a = divmod(t, QUAD)
-            rows = xd[d][:, a, :]
-            if engine == "V":
-                for i in range(2):
-                    nc.vector.bn_stats(out=xst[:, t, i, :], in_=rows[:, i * NH : (i + 1) * NH])
-            else:
-                i = state["g_next"]
-                state["g_next"] = i + 1
-                if fence_chunk is not None:
-                    nc.gpsimd.memset(grp[fence_chunk][:, 0:16], 0.0)
+                for h in range(2):
+                    nc.vector.bn_stats(out=xst[:, t, h, :], in_=xd_rows(t)[:, h * NH : (h + 1) * NH])
+
+        def squares_s(n):
+            for i in range(n):
+                t = rest[state["xd_next"]]
+                state["xd_next"] += 1
+                nc.scalar.activation(out=xd_rows(t), in_=xd_rows(t), func=ACT.Square, accum_out=xst[:, t, 0, 2:3])
+
+        def squares_g(tiles):
+            sq = {}
+            for t in tiles:
                 gsq = gsqp.tile([P, K], F32, name="gsq", tag="gsq")
-                nc.gpsimd.tensor_tensor(out=gsq[:], in0=rows, in1=rows, op=ALU.mult)
-                nc.gpsimd.tensor_tensor(out=gsq[:, 0:512], in0=gsq[:, 0:512], in1=gsq[:, 512:1024], op=ALU.add)
-                nc.gpsimd.tensor_tensor(out=gsq[:, 0:256], in0=gsq[:, 0:256], in1=gsq[:, 256:512], op=ALU.add)
-                nc.gpsimd.tensor_tensor(out=gacc[:, i, :], in0=gsq[:, 0:128], in1=gsq[:, 128:256], op=ALU.add)
+                sq[t] = gsq
+                nc.gpsimd.tensor_tensor(out=gsq[:], in0=xd_rows(t), in1=xd_rows(t), op=ALU.mult)
+            for t in tiles:
+                nc.gpsimd.tensor_tensor(out=sq[t][:, 0:512], in0=sq[t][:, 0:512], in1=sq[t][:, 512:1024], op=ALU.add)
+            for t in tiles:
+                nc.gpsimd.tensor_tensor(
+                    out=gacc[:, G_LIST.index(t), :], in0=sq[t][:, 0:256], in1=sq[t][:, 256:512], op=ALU.add
+                )
 
         def keep_clock(n):
-            idle = ps_m.tile([P, NH], F32, name="idle", tag="acc")
+            idle = ps.tile([P, NH], F32, name="idle", tag="bank")
             for i in range(n):
                 nc.tensor.matmul(out=idle[:], lhsT=zeros[:, 0:P], rhs=zeros[:], start=(i == 0), stop=(i == n - 1))
 
@@ -221,25 +225,23 @@ def tile_scoremagnitudemetric_kernel(tc, x, x_dot, pos_sample, W, out):
         load_rows(1, 0, 2)
         load_w(1, 1)
         load_rows(1, 2, 2)
-        for kind, i in (
-            ("x", 2), ("x", 3), ("d", 0), ("x", 4), ("x", 5), ("d", 1), ("d", 2),
-        ):
-            if kind == "x":
-                load_rows(i, 0, QUAD)
-            else:
-                load_xd(i)
+        load_xd(0)
+        load_rows(2, 0, QUAD)
+        load_rows(3, 0, QUAD)
+        load_rows(4, 0, QUAD)
+        load_xd(1)
+        load_rows(5, 0, QUAD)
 
         regroup_w(0, RG_SPLIT, NH, "S")
         regroup_w(0, 0, RG_SPLIT, "V")
-        quantise_w(0, 0)
         regroup_w(1, RG_SPLIT, NH, "S")
         regroup_w(1, 0, RG_SPLIT, "V")
+        quantise_w(0, 0)
         quantise_w(1, 0)
 
         keep_clock(WARM_FIRST)
         transposes(0)
         transposes(1)
-        keep_clock(1)
         copy_out(0, False)
         quantise(0, 0, 1)
         copy_out(1, False)
@@ -251,31 +253,28 @@ def tile_scoremagnitudemetric_kernel(tc, x, x_dot, pos_sample, W, out):
         scores(0, 0)
         scores(1, 0)
         quantise(0, 2, 2)
+        regroup_w(0, NH, NH + RG_G, "V")
+        regroup_w(0, NH + RG_G, N, "G")
         transposes(4)
         transposes(5)
         copy_out(4, True)
         copy_out(5, True)
         scores(2, 0)
         scores(3, 0)
+        regroup_w(1, NH, NH + RG_G, "V")
         quantise(1, 0, 2)
+        quantise_w(0, 1)
         transposes(6)
         transposes(7)
-        copy_out(6, True)
+        copy_out(6, False)
         copy_out(7, False)
+        regroup_w(1, NH + RG_G, N, "G")
         scores(4, 0)
         scores(5, 0)
         quantise(1, 2, 2)
-        for g in range(2):
-            for n0 in range(NH, N, RG_PIECE):
-                regroup_w(g, n0, n0 + RG_PIECE, "G")
-            quantise_w(g, 1)
+        quantise_w(1, 1)
         scores(6, 0)
         scores(7, 0)
-        def transpose_group(g):
-            for i in range(OCT):
-                transposes(OCT * g + i)
-            for i in range(OCT):
-                copy_out(OCT * g + i, i not in S_COPIES)
 
         n_pos = small[:, 0:8]
         loc_max = small[:, 16:17]
@@ -288,72 +287,96 @@ def tile_scoremagnitudemetric_kernel(tc, x, x_dot, pos_sample, W, out):
         alpha = small[:, 21:22]
         beta = small[:, 22:23]
 
+        def turn(chunks, s_copies, n_s):
+            tiles = [QUAD * c + a for c in chunks for a in range(QUAD)]
+            for j in tiles:
+                transposes(j)
+            squares_s(n_s)
+            for i, j in enumerate(tiles):
+                copy_out(j, i not in s_copies)
+
+        def quantise_all(chunks):
+            for c in chunks:
+                quantise(c, 0, QUAD)
+
+        def multiply(chunks):
+            for c in chunks:
+                for a in range(QUAD):
+                    for h in range(2):
+                        scores(QUAD * c + a, h)
+
         load_rows(6, 0, QUAD)
+        load_xd(2)
         load_rows(7, 0, QUAD)
         load_xd(3)
-        load_xd(4)
-        transpose_group(1)
-        load_rows(8, 0, QUAD)
-        load_rows(9, 0, QUAD)
-        for j in range(POS_TILES):
+        squares_v(2)
+        for j in range(4):
             scores(j, 1)
-        quantise(2, 0, QUAD)
-        quantise(3, 0, QUAD)
-        for i in range(XG[0]):
-            xdot("G", None)
-        for i in range(XV[0]):
-            xdot("V")
+        turn((2,), (0,), 0)
+        load_rows(8, 0, QUAD)
+        load_xd(4)
+        load_xd(5)
+        for i in range(0, 8, 2):
+            squares_g(G_LIST[i : i + 2])
+        quantise_all((2,))
+        for j in range(4, POS_TILES):
+            scores(j, 1)
 
-        for p in range(1, GROUPS + 1):
-            if p < GROUPS:
-                transpose_group(p + 1)
-                quantise(2 * p + 2, 0, QUAD)
-                quantise(2 * p + 3, 0, QUAD)
-            else:
-                stat = ps_t.tile([P, 4, P], F32, name="stat", tag="tp")
-                nc.tensor.transpose(stat[:, 0, :], loc_max.to_broadcast([P, P]), ident[:])
-                nc.tensor.transpose(stat[:, 1, :], loc_min.to_broadcast([P, P]), ident[:])
-                nc.vector.tensor_reduce(out=g_max, in_=stat[:, 0, :], axis=AX.X, op=ALU.max)
-                nc.vector.tensor_reduce(out=g_min, in_=stat[:, 1, :], axis=AX.X, op=ALU.min)
-                nc.vector.tensor_tensor(out=small[:, 24:26], in0=small[:, 18:20], in1=small[:, 18:20], op=ALU.mult)
-                nc.vector.tensor_tensor(out=span, in0=g4_max, in1=g4_min, op=ALU.subtract)
-                nc.vector.reciprocal(out=span, in_=span)
-                nc.vector.tensor_scalar(out=alpha, in0=span, scalar1=MAXI - MINI, scalar2=None, op0=ALU.mult)
-                nc.vector.tensor_tensor(out=beta, in0=alpha, in1=g4_min, op=ALU.mult)
-                nc.vector.tensor_scalar(out=beta, in0=beta, scalar1=-1.0, scalar2=MINI, op0=ALU.mult, op1=ALU.add)
-            for i in range(XG[p]):
-                xdot("G", None)
-            for i in range(XV[p]):
-                xdot("V")
-            if p == 1:
-                load_xd(5)
-            if p == 2:
-                load_xd(6)
-                load_xd(7)
-            if p == 1:
-                nc.vector.tensor_reduce(out=n_pos, in_=ssq[:, 0:POS_TILES, :], axis=AX.X, op=ALU.add)
-                nc.vector.tensor_reduce(out=loc_max, in_=n_pos, axis=AX.X, op=ALU.max)
-                nc.vector.tensor_reduce(out=loc_min, in_=n_pos, axis=AX.X, op=ALU.min)
-            if p == 3:
-                nc.vector.tensor_reduce(
-                    out=xst[:].rearrange("p (d a) i v -> p d a i v", a=QUAD)[:, 0:5, 1, 0, 2], in_=gacc[:, 0:5, :], axis=AX.X, op=ALU.add
-                )
-            if p == GROUPS:
-                nc.vector.tensor_reduce(
-                    out=xst[:].rearrange("p (d a) i v -> p d a i v", a=QUAD)[:, 5:8, 1, 0, 2], in_=gacc[:, 5:8, :], axis=AX.X, op=ALU.add
-                )
-                nc.vector.tensor_reduce(out=xst[:, 31, 0, 2:3], in_=gacc[:, 8:9, :], axis=AX.X, op=ALU.add)
-                trip = xst[:].rearrange("p t i (e v) -> p (t i e) v", v=3)
-                nc.vector.tensor_tensor(out=xtmp[:, 0, :], in0=trip[:, :, 1], in1=trip[:, :, 1], op=ALU.mult)
-                nc.vector.scalar_tensor_tensor(
-                    out=xtmp[:, 1, :], in0=xtmp[:, 0, :], scalar=float(NH // 2), in1=trip[:, :, 2], op0=ALU.mult, op1=ALU.add
-                )
-                nc.vector.tensor_reduce(
-                    out=fin[:, 0, :], in_=xtmp[:, 1, :].rearrange("p (t f) -> p t f", f=4), axis=AX.X, op=ALU.add
-                )
-            for i in range(OCT):
-                for h in range(2):
-                    scores(OCT * p + i, h)
+        turn((3, 4), (5, 6, 7), 1)
+        load_rows(9, 0, QUAD)
+        quantise_all((3, 4))
+        squares_v(1)
+        multiply((2,))
+        nc.vector.tensor_reduce(out=n_pos, in_=ssq[:, 0:POS_TILES, :], axis=AX.X, op=ALU.add)
+
+        turn((5, 6), (5, 6, 7), 1)
+        nc.vector.tensor_reduce(out=loc_max, in_=n_pos, axis=AX.X, op=ALU.max)
+        nc.vector.tensor_reduce(out=loc_min, in_=n_pos, axis=AX.X, op=ALU.min)
+        quantise_all((5, 6))
+        squares_v(5)
+        load_xd(6)
+        squares_g(G_LIST[8:10])
+        multiply((3, 4))
+
+        turn((7, 8), (5, 6, 7), 0)
+        stat = ps.tile([P, 4, P], F32, name="stat", tag="bank")
+        nc.tensor.transpose(stat[:, 0, :], loc_max.to_broadcast([P, P]), ident[:])
+        nc.tensor.transpose(stat[:, 1, :], loc_min.to_broadcast([P, P]), ident[:])
+        nc.vector.tensor_reduce(out=g_max, in_=stat[:, 0, :], axis=AX.X, op=ALU.max)
+        nc.vector.tensor_reduce(out=g_min, in_=stat[:, 1, :], axis=AX.X, op=ALU.min)
+        quantise_all((7, 8))
+        squares_v(6)
+        load_xd(7)
+        squares_g(G_LIST[10:11])
+        multiply((5, 6))
+
+        turn((9,), (), 0)
+        nc.vector.tensor_tensor(out=small[:, 24:26], in0=small[:, 18:20], in1=small[:, 18:20], op=ALU.mult)
+        quantise_all((9,))
+        nc.vector.tensor_tensor(out=span, in0=g4_max, in1=g4_min, op=ALU.subtract)
+        nc.vector.reciprocal(out=span, in_=span)
+        squares_v(1)
+        nc.vector.tensor_scalar(out=alpha, in0=span, scalar1=MAXI - MINI, scalar2=None, op0=ALU.mult)
+        squares_v(1)
+        nc.vector.tensor_tensor(out=beta, in0=alpha, in1=g4_min, op=ALU.mult)
+        squares_v(1)
+        nc.vector.tensor_scalar(out=beta, in0=beta, scalar1=-1.0, scalar2=MINI, op0=ALU.mult, op1=ALU.add)
+        multiply((7, 8))
+
+        by_four = xst[:].rearrange("p (d a) i v -> p d a i v", a=QUAD)
+        by_two = xst[:].rearrange("p (d a) i v -> p d a i v", a=2)
+        nc.vector.tensor_reduce(out=by_two[:, 0:7, 1, 0, 2], in_=gacc[:, 0:7, :], axis=AX.X, op=ALU.add)
+        squares_v(2)
+        nc.vector.tensor_reduce(out=by_four[:, 4:8, 1, 0, 2], in_=gacc[:, 7:11, :], axis=AX.X, op=ALU.add)
+        trip = xst[:].rearrange("p t i (e v) -> p (t i e) v", v=3)
+        nc.vector.tensor_tensor(out=xtmp[:, 0, :], in0=trip[:, :, 1], in1=trip[:, :, 1], op=ALU.mult)
+        nc.vector.scalar_tensor_tensor(
+            out=xtmp[:, 1, :], in0=xtmp[:, 0, :], scalar=float(NH // 2), in1=trip[:, :, 2], op0=ALU.mult, op1=ALU.add
+        )
+        nc.vector.tensor_reduce(
+            out=fin[:, 0, :], in_=xtmp[:, 1, :].rearrange("p (t f) -> p t f", f=4), axis=AX.X, op=ALU.add
+        )
+        multiply((9,))
 
         nc.vector.tensor_tensor(
             out=fin[:, 1, :], in0=ssq[:, POS_TILES:TILES, 0], in1=ssq[:, POS_TILES:TILES, 1], op=ALU.add

@@ -30,7 +30,7 @@ FLOPS = 2 * (B + NPOS) * K * N
 
 S_COPIES = (0, 3, 5)
 OCT = 8
-G_LIST = (1, 3, 5, 7, 9, 11, 13, 17, 21, 25, 29)
+G_LIST = (1, 3, 5, 7, 9, 11, 17, 21, 25, 29)
 G_TILES = len(G_LIST)
 RG_G = 320
 G_KEEP = 256
@@ -47,7 +47,7 @@ def tile_scoremagnitudemetric_kernel(tc, x, x_dot, pos_sample, W, out):
         grpp = ctx.enter_context(tc.tile_pool(name="grpp", bufs=4))
         codep = ctx.enter_context(tc.tile_pool(name="codep", bufs=5))
         junkp = ctx.enter_context(tc.tile_pool(name="junkp", bufs=4))
-        gsqp = ctx.enter_context(tc.tile_pool(name="gsqp", bufs=3))
+        gsqp = ctx.enter_context(tc.tile_pool(name="gsqp", bufs=2))
         ps = ctx.enter_context(tc.psum_pool(name="ps", bufs=8))
         ctx.enter_context(tc.manual_schedule())
 
@@ -193,16 +193,12 @@ def tile_scoremagnitudemetric_kernel(tc, x, x_dot, pos_sample, W, out):
                 nc.scalar.activation(out=xd_rows(t), in_=xd_rows(t), func=ACT.Square, accum_out=xst[:, t, 0, 2:3])
 
         def squares_g(tiles):
-            sq = {}
             for t in tiles:
                 gsq = gsqp.tile([P, K], F32, name="gsq", tag="gsq")
-                sq[t] = gsq
                 nc.gpsimd.tensor_tensor(out=gsq[:], in0=xd_rows(t), in1=xd_rows(t), op=ALU.mult)
-            for t in tiles:
-                nc.gpsimd.tensor_tensor(out=sq[t][:, 0:512], in0=sq[t][:, 0:512], in1=sq[t][:, 512:1024], op=ALU.add)
-            for t in tiles:
+                nc.gpsimd.tensor_tensor(out=gsq[:, 0:512], in0=gsq[:, 0:512], in1=gsq[:, 512:1024], op=ALU.add)
                 nc.gpsimd.tensor_tensor(
-                    out=gacc[:, G_LIST.index(t), :], in0=sq[t][:, 0:256], in1=sq[t][:, 256:512], op=ALU.add
+                    out=gacc[:, G_LIST.index(t), :], in0=gsq[:, 0:256], in1=gsq[:, 256:512], op=ALU.add
                 )
 
         def keep_clock(n):
@@ -316,8 +312,7 @@ def tile_scoremagnitudemetric_kernel(tc, x, x_dot, pos_sample, W, out):
         load_rows(8, 0, QUAD)
         load_xd(4)
         load_xd(5)
-        for i in range(0, 8, 2):
-            squares_g(G_LIST[i : i + 2])
+        squares_g(G_LIST[0:7])
         quantise_all((2,))
         for j in range(4, POS_TILES):
             scores(j, 1)
@@ -335,7 +330,7 @@ def tile_scoremagnitudemetric_kernel(tc, x, x_dot, pos_sample, W, out):
         quantise_all((5, 6))
         squares_v(5)
         load_xd(6)
-        squares_g(G_LIST[8:10])
+        squares_g(G_LIST[7:9])
         multiply((3, 4))
 
         turn((7, 8), (5, 6, 7), 0)
@@ -347,7 +342,7 @@ def tile_scoremagnitudemetric_kernel(tc, x, x_dot, pos_sample, W, out):
         quantise_all((7, 8))
         squares_v(6)
         load_xd(7)
-        squares_g(G_LIST[10:11])
+        squares_g(G_LIST[9:10])
         multiply((5, 6))
 
         turn((9,), (), 0)
@@ -365,9 +360,9 @@ def tile_scoremagnitudemetric_kernel(tc, x, x_dot, pos_sample, W, out):
 
         by_four = xst[:].rearrange("p (d a) i v -> p d a i v", a=QUAD)
         by_two = xst[:].rearrange("p (d a) i v -> p d a i v", a=2)
-        nc.vector.tensor_reduce(out=by_two[:, 0:7, 1, 0, 2], in_=gacc[:, 0:7, :], axis=AX.X, op=ALU.add)
-        squares_v(2)
-        nc.vector.tensor_reduce(out=by_four[:, 4:8, 1, 0, 2], in_=gacc[:, 7:11, :], axis=AX.X, op=ALU.add)
+        nc.vector.tensor_reduce(out=by_two[:, 0:6, 1, 0, 2], in_=gacc[:, 0:6, :], axis=AX.X, op=ALU.add)
+        squares_v(3)
+        nc.vector.tensor_reduce(out=by_four[:, 4:8, 1, 0, 2], in_=gacc[:, 6:10, :], axis=AX.X, op=ALU.add)
         trip = xst[:].rearrange("p t i (e v) -> p (t i e) v", v=3)
         nc.vector.tensor_tensor(out=xtmp[:, 0, :], in0=trip[:, :, 1], in1=trip[:, :, 1], op=ALU.mult)
         nc.vector.scalar_tensor_tensor(

@@ -30,7 +30,7 @@ FLOPS = 2 * (B + NPOS) * K * N
 
 S_COPIES = (0, 3, 5)
 OCT = 8
-G_LIST = (1, 3, 5, 7, 9, 11, 17, 21, 25, 29)
+G_LIST = (1, 5, 9, 13, 17, 21, 25)
 G_TILES = len(G_LIST)
 RG_G = 320
 G_KEEP = 256
@@ -192,7 +192,9 @@ def tile_scoremagnitudemetric_kernel(tc, x, x_dot, pos_sample, W, out):
                 state["xd_next"] += 1
                 nc.scalar.activation(out=xd_rows(t), in_=xd_rows(t), func=ACT.Square, accum_out=xst[:, t, 0, 2:3])
 
-        def squares_g(tiles):
+        def squares_g(tiles, fence=None):
+            if fence is not None:
+                nc.gpsimd.memset(grp[fence][:, 0:16], 0.0)
             for t in tiles:
                 gsq = gsqp.tile([P, K], F32, name="gsq", tag="gsq")
                 nc.gpsimd.tensor_tensor(out=gsq[:], in0=xd_rows(t), in1=xd_rows(t), op=ALU.mult)
@@ -305,21 +307,22 @@ def tile_scoremagnitudemetric_kernel(tc, x, x_dot, pos_sample, W, out):
         load_xd(2)
         load_rows(7, 0, QUAD)
         load_xd(3)
+        squares_g(G_LIST[0:1])
         squares_v(2)
-        for j in range(4):
+        for j in range(2):
             scores(j, 1)
-        turn((2,), (0,), 0)
+        turn((2,), (0,), 1)
         load_rows(8, 0, QUAD)
         load_xd(4)
         load_xd(5)
-        squares_g(G_LIST[0:7])
         quantise_all((2,))
-        for j in range(4, POS_TILES):
+        for j in range(2, POS_TILES):
             scores(j, 1)
 
         turn((3, 4), (5, 6, 7), 1)
         load_rows(9, 0, QUAD)
         quantise_all((3, 4))
+        squares_g(G_LIST[1:2], 4)
         squares_v(1)
         multiply((2,))
         nc.vector.tensor_reduce(out=n_pos, in_=ssq[:, 0:POS_TILES, :], axis=AX.X, op=ALU.add)
@@ -328,41 +331,39 @@ def tile_scoremagnitudemetric_kernel(tc, x, x_dot, pos_sample, W, out):
         nc.vector.tensor_reduce(out=loc_max, in_=n_pos, axis=AX.X, op=ALU.max)
         nc.vector.tensor_reduce(out=loc_min, in_=n_pos, axis=AX.X, op=ALU.min)
         quantise_all((5, 6))
-        squares_v(5)
+        squares_g(G_LIST[2:4], 6)
+        squares_v(6)
         load_xd(6)
-        squares_g(G_LIST[7:9])
         multiply((3, 4))
 
-        turn((7, 8), (5, 6, 7), 0)
+        turn((7, 8), (5, 6, 7), 1)
         stat = ps.tile([P, 4, P], F32, name="stat", tag="bank")
         nc.tensor.transpose(stat[:, 0, :], loc_max.to_broadcast([P, P]), ident[:])
         nc.tensor.transpose(stat[:, 1, :], loc_min.to_broadcast([P, P]), ident[:])
         nc.vector.tensor_reduce(out=g_max, in_=stat[:, 0, :], axis=AX.X, op=ALU.max)
         nc.vector.tensor_reduce(out=g_min, in_=stat[:, 1, :], axis=AX.X, op=ALU.min)
         quantise_all((7, 8))
-        squares_v(6)
+        squares_g(G_LIST[4:6], 8)
+        squares_v(5)
         load_xd(7)
-        squares_g(G_LIST[9:10])
         multiply((5, 6))
+        nc.scalar.activation(out=small[:, 24:26], in_=small[:, 18:20], func=ACT.Square)
 
         turn((9,), (), 0)
-        nc.vector.tensor_tensor(out=small[:, 24:26], in0=small[:, 18:20], in1=small[:, 18:20], op=ALU.mult)
-        quantise_all((9,))
-        nc.vector.tensor_tensor(out=span, in0=g4_max, in1=g4_min, op=ALU.subtract)
+        nc.vector.tensor_scalar(out=span, in0=g4_max, scalar1=g4_min, scalar2=None, op0=ALU.subtract)
         nc.vector.reciprocal(out=span, in_=span)
-        squares_v(1)
         nc.vector.tensor_scalar(out=alpha, in0=span, scalar1=MAXI - MINI, scalar2=None, op0=ALU.mult)
-        squares_v(1)
-        nc.vector.tensor_tensor(out=beta, in0=alpha, in1=g4_min, op=ALU.mult)
-        squares_v(1)
-        nc.vector.tensor_scalar(out=beta, in0=beta, scalar1=-1.0, scalar2=MINI, op0=ALU.mult, op1=ALU.add)
+        nc.vector.tensor_scalar(out=beta, in0=alpha, scalar1=g4_min, scalar2=-1.0, op0=ALU.mult, op1=ALU.mult)
+        quantise_all((9,))
+        squares_g(G_LIST[6:7], 9)
+        nc.vector.tensor_scalar(out=beta, in0=beta, scalar1=MINI, scalar2=None, op0=ALU.add)
+        squares_v(4)
         multiply((7, 8))
 
         by_four = xst[:].rearrange("p (d a) i v -> p d a i v", a=QUAD)
-        by_two = xst[:].rearrange("p (d a) i v -> p d a i v", a=2)
-        nc.vector.tensor_reduce(out=by_two[:, 0:6, 1, 0, 2], in_=gacc[:, 0:6, :], axis=AX.X, op=ALU.add)
+        nc.vector.tensor_reduce(out=by_four[:, 0:6, 1, 0, 2], in_=gacc[:, 0:6, :], axis=AX.X, op=ALU.add)
         squares_v(3)
-        nc.vector.tensor_reduce(out=by_four[:, 4:8, 1, 0, 2], in_=gacc[:, 6:10, :], axis=AX.X, op=ALU.add)
+        nc.vector.tensor_reduce(out=by_four[:, 6:7, 1, 0, 2], in_=gacc[:, 6:7, :], axis=AX.X, op=ALU.add)
         trip = xst[:].rearrange("p t i (e v) -> p (t i e) v", v=3)
         nc.vector.tensor_tensor(out=xtmp[:, 0, :], in0=trip[:, :, 1], in1=trip[:, :, 1], op=ALU.mult)
         nc.vector.scalar_tensor_tensor(

@@ -284,6 +284,9 @@ def tile_scoremagnitudemetric_kernel(tc, x, x_dot, pos_sample, W, out):
         span = small[:, 20:21]
         alpha = small[:, 21:22]
         beta = small[:, 22:23]
+        last_scale = small[:, 32:33]
+        last_shift = small[:, 33:34]
+        last_square = small[:, 40:41]
 
         def turn(chunks, s_copies, n_s):
             tiles = [QUAD * c + a for c in chunks for a in range(QUAD)]
@@ -308,22 +311,20 @@ def tile_scoremagnitudemetric_kernel(tc, x, x_dot, pos_sample, W, out):
         load_rows(7, 0, QUAD)
         load_xd(3)
         squares_g(G_LIST[0:1])
-        squares_v(2)
-        for j in range(2):
+        squares_v(3)
+        for j in range(POS_TILES):
             scores(j, 1)
-        turn((2,), (0,), 1)
+        turn((2,), (), 0)
+        turn((3,), (0, 1, 2, 3), 0)
+        quantise_all((2,))
+        turn((4,), (2, 3), 0)
         load_rows(8, 0, QUAD)
         load_xd(4)
         load_xd(5)
-        quantise_all((2,))
-        for j in range(2, POS_TILES):
-            scores(j, 1)
-
-        turn((3, 4), (5, 6, 7), 1)
         load_rows(9, 0, QUAD)
         quantise_all((3, 4))
         squares_g(G_LIST[1:2], 4)
-        squares_v(1)
+        squares_v(2)
         multiply((2,))
         nc.vector.tensor_reduce(out=n_pos, in_=ssq[:, 0:POS_TILES, :], axis=AX.X, op=ALU.add)
 
@@ -344,7 +345,7 @@ def tile_scoremagnitudemetric_kernel(tc, x, x_dot, pos_sample, W, out):
         nc.vector.tensor_reduce(out=g_min, in_=stat[:, 1, :], axis=AX.X, op=ALU.min)
         quantise_all((7, 8))
         squares_g(G_LIST[4:6], 8)
-        squares_v(5)
+        squares_v(6)
         load_xd(7)
         multiply((5, 6))
         nc.scalar.activation(out=small[:, 24:26], in_=small[:, 18:20], func=ACT.Square)
@@ -362,7 +363,7 @@ def tile_scoremagnitudemetric_kernel(tc, x, x_dot, pos_sample, W, out):
 
         by_four = xst[:].rearrange("p (d a) i v -> p d a i v", a=QUAD)
         nc.vector.tensor_reduce(out=by_four[:, 0:6, 1, 0, 2], in_=gacc[:, 0:6, :], axis=AX.X, op=ALU.add)
-        squares_v(3)
+        squares_v(2)
         nc.vector.tensor_reduce(out=by_four[:, 6:7, 1, 0, 2], in_=gacc[:, 6:7, :], axis=AX.X, op=ALU.add)
         trip = xst[:].rearrange("p t i (e v) -> p (t i e) v", v=3)
         nc.vector.tensor_tensor(out=xtmp[:, 0, :], in0=trip[:, :, 1], in1=trip[:, :, 1], op=ALU.mult)
@@ -372,15 +373,24 @@ def tile_scoremagnitudemetric_kernel(tc, x, x_dot, pos_sample, W, out):
         nc.vector.tensor_reduce(
             out=fin[:, 0, :], in_=xtmp[:, 1, :].rearrange("p (t f) -> p t f", f=4), axis=AX.X, op=ALU.add
         )
+        last = X_TILES - 1
+        nc.vector.tensor_scalar(out=last_scale, in0=fin[:, 0, last:], scalar1=alpha, scalar2=None, op0=ALU.mult)
+        nc.vector.tensor_scalar(out=last_shift, in0=fin[:, 0, last:], scalar1=beta, scalar2=None, op0=ALU.mult)
         multiply((9,))
 
         nc.vector.tensor_tensor(
-            out=fin[:, 1, :], in0=ssq[:, POS_TILES:TILES, 0], in1=ssq[:, POS_TILES:TILES, 1], op=ALU.add
+            out=fin[:, 1, 0:last], in0=ssq[:, POS_TILES : TILES - 1, 0], in1=ssq[:, POS_TILES : TILES - 1, 1], op=ALU.add
         )
         nc.vector.scalar_tensor_tensor(
-            out=fin[:, 2, :], in0=fin[:, 1, :], scalar=alpha, in1=fin[:, 1, :], op0=ALU.mult, op1=ALU.mult
+            out=fin[:, 2, 0:last], in0=fin[:, 1, 0:last], scalar=alpha, in1=fin[:, 1, 0:last], op0=ALU.mult, op1=ALU.mult
         )
         nc.vector.scalar_tensor_tensor(
-            out=fin[:, 3, :], in0=fin[:, 2, :], scalar=beta, in1=fin[:, 0, :], op0=ALU.add, op1=ALU.mult
+            out=fin[:, 3, 0:last], in0=fin[:, 2, 0:last], scalar=beta, in1=fin[:, 0, 0:last], op0=ALU.add, op1=ALU.mult
+        )
+        nc.scalar.activation(
+            out=last_square, in_=ssq[:, TILES - 1, 1:2], func=ACT.Square, bias=ssq[:, TILES - 1, 0:1]
+        )
+        nc.vector.tensor_scalar(
+            out=fin[:, 3, last:], in0=last_square, scalar1=last_scale, scalar2=last_shift, op0=ALU.mult, op1=ALU.add
         )
         nc.sync.dma_start(out=out_v, in_=fin[:, 3, :])

from contextlib import ExitStack

import concourse.mybir as mybir
from concourse.masks import make_identity

F32 = mybir.dt.float32
BF16 = mybir.dt.bfloat16
U32 = mybir.dt.uint32
U8 = mybir.dt.uint8
FP8X4 = mybir.dt.float8_e4m3fn_x4
ACT = mybir.ActivationFunctionType
ALU = mybir.AluOpType
AX = mybir.AxisListType

P = 128
K = 1024
N = 1024
NH = 512
B = 4096
NPOS = 1024
QUAD = 4
POS_TILES = NPOS // P
X_TILES = B // P
TILES = POS_TILES + X_TILES
CHUNKS = TILES // QUAD
MINI = 0.001
MAXI = 1.0

FLOPS = 2 * (B + NPOS) * K * N

S_COPIES = (0, 3, 5)
OCT = 8
G_LIST = (1, 5, 9, 13, 17, 21, 25)
G_TILES = len(G_LIST)
RG_G = 320
G_KEEP = 256
WARM_FIRST = 10
RG_SPLIT = 336


def tile_scoremagnitudemetric_kernel(tc, x, x_dot, pos_sample, W, out):
    nc = tc.nc
    with ExitStack() as ctx:
        const = ctx.enter_context(tc.tile_pool(name="const", bufs=1))
        rawp = ctx.enter_context(tc.tile_pool(name="rawp", bufs=6))
        xdp = ctx.enter_context(tc.tile_pool(name="xdp", bufs=6))
        grpp = ctx.enter_context(tc.tile_pool(name="grpp", bufs=4))
        codep = ctx.enter_context(tc.tile_pool(name="codep", bufs=5))
        junkp = ctx.enter_context(tc.tile_pool(name="junkp", bufs=4))
        gsqp = ctx.enter_context(tc.tile_pool(name="gsqp", bufs=2))
        ps = ctx.enter_context(tc.psum_pool(name="ps", bufs=8))
        ctx.enter_context(tc.manual_schedule())

        pos_v = pos_sample.rearrange("(p t) k -> p t k", t=POS_TILES)
        x_v = x.rearrange("(p t) k -> p t k", t=X_TILES)
        xd_v = x_dot.rearrange("(p t) k -> p t k", t=X_TILES)
        out_v = out.rearrange("(p t) -> p t", t=X_TILES)

        ident = const.tile([P, P], F32, name="ident")
        w_raw = {}
        for g in range(2):
            for h in range(2):
                w_piece = const.tile([P, 4, NH], BF16, name="w_piece", tag="w_raw%d%d" % (g, h))
                w_raw[(g, h)] = w_piece
        w_grp = const.tile([P, 2, N, 4], BF16, name="w_grp", align_bytes=64)
        w_codes = const.tile([P, 2 * N], U32, name="w_codes", align_bytes=64)
        w_scales = const.tile([P, 2 * N], U8, name="w_scales", align_bytes=64)
        ssq = const.tile([P, TILES, 2], F32, name="ssq")
        xst = const.tile([P, X_TILES, 2, 6], F32, name="xst")
        xtmp = const.tile([P, 2, 4 * X_TILES], F32, name="xtmp")
        gacc = const.tile([P, G_TILES, G_KEEP], F32, name="gacc")
        warm = const.tile([P, 1], F32, name="warm")
        zeros = const.tile([P, NH], BF16, name="zeros")
        small = const.tile([P, 64], F32, name="small")
        fin = const.tile([P, 4, X_TILES], F32, name="fin")

        raw = {}
        xd = {}
        grp = {}
        codes = {}
        scales = {}
        tps = {}
        state = {"xd_next": 0}
        rest = [t for t in range(X_TILES) if t not in G_LIST]

        def load_w(g, h):
            for u in range(2):
                r0 = 512 * g + 256 * u
                nc.sync.dma_start(
                    out=w_raw[(g, h)][:, 2 * u : 2 * u + 2, :],
                    in_=W[r0 : r0 + 256, h * NH : (h + 1) * NH].rearrange("(q e) c -> q e c", e=2),
                )

        def load_rows(c, a0, n):
            if a0 == 0:
                raw_t = rawp.tile([P, QUAD, K], BF16, name="raw_t", tag="raw")
                raw[c] = raw_t
            if c < 2:
                src = pos_v[:, QUAD * c + a0 : QUAD * c + a0 + n, :]
            else:
                src = x_v[:, QUAD * (c - 2) + a0 : QUAD * (c - 2) + a0 + n, :]
            nc.sync.dma_start(out=raw[c][:, a0 : a0 + n, :], in_=src)

        def load_xd(d):
            xd_t = xdp.tile([P, QUAD, K], BF16, name="xd_t", tag="xd")
            xd[d] = xd_t
            nc.sync.dma_start(out=xd_t[:], in_=xd_v[:, QUAD * d : QUAD * (d + 1), :])

        def regroup_w(g, n0, n1, on_vector):
            dst = w_grp[:, g, n0:n1, :].rearrange("p (c i) t -> p c t i", i=4)
            h = n0 // NH
            src = w_raw[(g, h)][:, :, n0 - h * NH : n1 - h * NH].rearrange("p t (c i) -> p c t i", i=4)
            if on_vector == "V":
                nc.vector.tensor_copy(out=dst, in_=src)
            elif on_vector == "S":
                nc.scalar.copy(out=dst, in_=src)
            else:
                nc.gpsimd.tensor_scalar(out=dst, in0=src, scalar1=1.0, scalar2=0.0, op0=ALU.mult, op1=ALU.add)

        def quantise_w(g, h):
            cols = slice(g * N + h * NH, g * N + (h + 1) * NH)
            nc.vector.quantize_mx(
                out=w_codes[:, cols].bitcast(FP8X4),
                scales=w_scales[:, cols],
                in_=w_grp[:, g, h * NH : (h + 1) * NH, :].rearrange("p n t -> p (n t)"),
            )

        def transposes(j):
            c, a = divmod(j, QUAD)
            tp = ps.tile([P, 4, P], F32, name="tp", tag="bank")
            tps[j] = tp
            words = raw[c][:, a, :].bitcast(F32)
            for q in range(4):
                nc.tensor.transpose(tp[:, q, :], words[:, q * P : (q + 1) * P], ident[:])

        def copy_out(j, on_vector):
            c, a = divmod(j, QUAD)
            if a == 0:
                grp_t = grpp.tile([P, QUAD * K], BF16, name="grp_t", tag="grp", align_bytes=64)
                grp[c] = grp_t
            dst = grp[c][:, a * K : (a + 1) * K].bitcast(F32).rearrange("p (g r u) -> p g r u", g=2, u=2)
            src = tps[j][:].rearrange("p (g u) r -> p g r u", g=2)
            if on_vector:
                nc.vector.tensor_copy(out=dst, in_=src)
            else:
                nc.scalar.copy(out=dst, in_=src)

        def quantise(c, a0, n):
            if a0 == 0:
                codes_t = codep.tile([P, QUAD * 256], U32, name="codes_t", tag="codes", align_bytes=64)
                scales_t = codep.tile([P, QUAD * 256], U8, name="scales_t", tag="scales", align_bytes=64)
                codes[c] = codes_t
                scales[c] = scales_t
            nc.vector.quantize_mx(
                out=codes[c][:, a0 * 256 : (a0 + n) * 256].bitcast(FP8X4),
                scales=scales[c][:, a0 * 256 : (a0 + n) * 256],
                in_=grp[c][:, a0 * K : (a0 + n) * K],
            )

        def scores(j, h):
            c, a = divmod(j, QUAD)
            acc = ps.tile([P, NH], F32, name="acc", tag="bank")
            for g in range(2):
                lcols = slice(a * 256 + g * P, a * 256 + (g + 1) * P)
                rcols = slice(g * N + h * NH, g * N + (h + 1) * NH)
                nc.tensor.matmul_mx(
                    out=acc[:],
                    lhsT=codes[c][:, lcols].bitcast(FP8X4),
                    lhsT_scale=scales[c][:, lcols],
                    rhs=w_codes[:, rcols].bitcast(FP8X4),
                    rhs_scale=w_scales[:, rcols],
                    start=(g == 0),
                    stop=(g == 1),
                )
            junk = junkp.tile([P, NH], BF16, name="junk", tag="junk")
            nc.scalar.activation(out=junk[:], in_=acc[:], func=ACT.Square, accum_out=ssq[:, j, h : h + 1])

        def xd_rows(t):
            d, a = divmod(t, QUAD)
            return xd[d][:, a, :]

        def squares_v(n):
            for i in range(n):
                t = rest[state["xd_next"]]
                state["xd_next"] += 1
                for h in range(2):
                    nc.vector.bn_stats(out=xst[:, t, h, :], in_=xd_rows(t)[:, h * NH : (h + 1) * NH])

        def squares_s(n):
            for i in range(n):
                t = rest[state["xd_next"]]
                state["xd_next"] += 1
                nc.scalar.activation(out=xd_rows(t), in_=xd_rows(t), func=ACT.Square, accum_out=xst[:, t, 0, 2:3])

        def squares_g(tiles, fence=None):
            if fence is not None:
                nc.gpsimd.memset(grp[fence][:, 0:16], 0.0)
            for t in tiles:
                gsq = gsqp.tile([P, K], F32, name="gsq", tag="gsq")
                nc.gpsimd.tensor_tensor(out=gsq[:], in0=xd_rows(t), in1=xd_rows(t), op=ALU.mult)
                nc.gpsimd.tensor_tensor(out=gsq[:, 0:512], in0=gsq[:, 0:512], in1=gsq[:, 512:1024], op=ALU.add)
                nc.gpsimd.tensor_tensor(
                    out=gacc[:, G_LIST.index(t), :], in0=gsq[:, 0:256], in1=gsq[:, 256:512], op=ALU.add
                )

        def keep_clock(n):
            idle = ps.tile([P, NH], F32, name="idle", tag="bank")
            for i in range(n):
                nc.tensor.matmul(out=idle[:], lhsT=zeros[:, 0:P], rhs=zeros[:], start=(i == 0), stop=(i == n - 1))

        nc.vector.memset(zeros[:], 0.0)
        make_identity(nc, ident[:])
        nc.vector.memset(warm[:], 0.0)
        nc.scalar.activation(out=warm[:], in_=warm[:], func=ACT.Square)
        nc.vector.memset(xst[:], 0.0)

        load_w(0, 0)
        load_w(1, 0)
        load_rows(0, 0, 1)
        load_rows(0, 1, 1)
        load_rows(0, 2, 2)
        load_w(0, 1)
        load_rows(1, 0, 2)
        load_w(1, 1)
        load_rows(1, 2, 2)
        load_xd(0)
        load_rows(2, 0, QUAD)
        load_rows(3, 0, QUAD)
        load_rows(4, 0, QUAD)
        load_xd(1)
        load_rows(5, 0, QUAD)

        regroup_w(0, RG_SPLIT, NH, "S")
        regroup_w(0, 0, RG_SPLIT, "V")
        regroup_w(1, RG_SPLIT, NH, "S")
        regroup_w(1, 0, RG_SPLIT, "V")
        quantise_w(0, 0)
        quantise_w(1, 0)

        keep_clock(WARM_FIRST)
        transposes(0)
        transposes(1)
        copy_out(0, False)
        quantise(0, 0, 1)
        copy_out(1, False)
        quantise(0, 1, 1)
        transposes(2)
        transposes(3)
        copy_out(2, True)
        copy_out(3, False)
        scores(0, 0)
        scores(1, 0)
        quantise(0, 2, 2)
        regroup_w(0, NH, NH + RG_G, "V")
        regroup_w(0, NH + RG_G, N, "G")
        transposes(4)
        transposes(5)
        copy_out(4, True)
        copy_out(5, True)
        scores(2, 0)
        scores(3, 0)
        regroup_w(1, NH, NH + RG_G, "V")
        quantise(1, 0, 2)
        quantise_w(0, 1)
        transposes(6)
        transposes(7)
        copy_out(6, False)
        copy_out(7, False)
        regroup_w(1, NH + RG_G, N, "G")
        scores(4, 0)
        scores(5, 0)
        quantise(1, 2, 2)
        quantise_w(1, 1)
        scores(6, 0)
        scores(7, 0)

        n_pos = small[:, 0:8]
        loc_max = small[:, 16:17]
        loc_min = small[:, 17:18]
        g_max = small[:, 18:19]
        g_min = small[:, 19:20]
        g4_max = small[:, 24:25]
        g4_min = small[:, 25:26]
        span = small[:, 20:21]
        alpha = small[:, 21:22]
        beta = small[:, 22:23]
        last_scale = small[:, 32:33]
        last_shift = small[:, 33:34]
        last_square = small[:, 40:41]

        def turn(chunks, s_copies, n_s):
            tiles = [QUAD * c + a for c in chunks for a in range(QUAD)]
            for j in tiles:
                transposes(j)
            squares_s(n_s)
            for i, j in enumerate(tiles):
                copy_out(j, i not in s_copies)

        def quantise_all(chunks):
            for c in chunks:
                quantise(c, 0, QUAD)

        def multiply(chunks):
            for c in chunks:
                for a in range(QUAD):
                    for h in range(2):
                        scores(QUAD * c + a, h)

        load_rows(6, 0, QUAD)
        load_xd(2)
        load_rows(7, 0, QUAD)
        load_xd(3)
        squares_g(G_LIST[0:1])
        squares_v(3)
        for j in range(POS_TILES):
            scores(j, 1)
        turn((2,), (), 0)
        turn((3,), (0, 1, 2, 3), 0)
        quantise_all((2,))
        turn((4,), (2, 3), 0)
        load_rows(8, 0, QUAD)
        load_xd(4)
        load_xd(5)
        load_rows(9, 0, QUAD)
        quantise_all((3, 4))
        squares_g(G_LIST[1:2], 4)
        squares_v(2)
        multiply((2,))
        nc.vector.tensor_reduce(out=n_pos, in_=ssq[:, 0:POS_TILES, :], axis=AX.X, op=ALU.add)

        turn((5, 6), (5, 6, 7), 1)
        nc.vector.tensor_reduce(out=loc_max, in_=n_pos, axis=AX.X, op=ALU.max)
        nc.vector.tensor_reduce(out=loc_min, in_=n_pos, axis=AX.X, op=ALU.min)
        quantise_all((5, 6))
        squares_g(G_LIST[2:4], 6)
        squares_v(6)
        load_xd(6)
        multiply((3, 4))

        turn((7, 8), (5, 6, 7), 1)
        stat = ps.tile([P, 4, P], F32, name="stat", tag="bank")
        nc.tensor.transpose(stat[:, 0, :], loc_max.to_broadcast([P, P]), ident[:])
        nc.tensor.transpose(stat[:, 1, :], loc_min.to_broadcast([P, P]), ident[:])
        nc.vector.tensor_reduce(out=g_max, in_=stat[:, 0, :], axis=AX.X, op=ALU.max)
        nc.vector.tensor_reduce(out=g_min, in_=stat[:, 1, :], axis=AX.X, op=ALU.min)
        quantise_all((7, 8))
        squares_g(G_LIST[4:6], 8)
        squares_v(6)
        load_xd(7)
        multiply((5, 6))
        nc.scalar.activation(out=small[:, 24:26], in_=small[:, 18:20], func=ACT.Square)

        turn((9,), (), 0)
        nc.vector.tensor_scalar(out=span, in0=g4_max, scalar1=g4_min, scalar2=None, op0=ALU.subtract)
        nc.vector.reciprocal(out=span, in_=span)
        nc.vector.tensor_scalar(out=alpha, in0=span, scalar1=MAXI - MINI, scalar2=None, op0=ALU.mult)
        nc.vector.tensor_scalar(out=beta, in0=alpha, scalar1=g4_min, scalar2=-1.0, op0=ALU.mult, op1=ALU.mult)
        quantise_all((9,))
        squares_g(G_LIST[6:7], 9)
        nc.vector.tensor_scalar(out=beta, in0=beta, scalar1=MINI, scalar2=None, op0=ALU.add)
        squares_v(4)
        multiply((7, 8))

        by_four = xst[:].rearrange("p (d a) i v -> p d a i v", a=QUAD)
        nc.vector.tensor_reduce(out=by_four[:, 0:6, 1, 0, 2], in_=gacc[:, 0:6, :], axis=AX.X, op=ALU.add)
        squares_v(2)
        nc.vector.tensor_reduce(out=by_four[:, 6:7, 1, 0, 2], in_=gacc[:, 6:7, :], axis=AX.X, op=ALU.add)
        trip = xst[:].rearrange("p t i (e v) -> p (t i e) v", v=3)
        nc.vector.tensor_tensor(out=xtmp[:, 0, :], in0=trip[:, :, 1], in1=trip[:, :, 1], op=ALU.mult)
        nc.vector.scalar_tensor_tensor(
            out=xtmp[:, 1, :], in0=xtmp[:, 0, :], scalar=float(NH // 2), in1=trip[:, :, 2], op0=ALU.mult, op1=ALU.add
        )
        nc.vector.tensor_reduce(
            out=fin[:, 0, :], in_=xtmp[:, 1, :].rearrange("p (t f) -> p t f", f=4), axis=AX.X, op=ALU.add
        )
        last = X_TILES - 1
        nc.vector.tensor_scalar(out=last_scale, in0=fin[:, 0, last:], scalar1=alpha, scalar2=None, op0=ALU.mult)
        nc.vector.tensor_scalar(out=last_shift, in0=fin[:, 0, last:], scalar1=beta, scalar2=None, op0=ALU.mult)
        multiply((9,))

        nc.vector.tensor_tensor(
            out=fin[:, 1, 0:last], in0=ssq[:, POS_TILES : TILES - 1, 0], in1=ssq[:, POS_TILES : TILES - 1, 1], op=ALU.add
        )
        nc.vector.scalar_tensor_tensor(
            out=fin[:, 2, 0:last], in0=fin[:, 1, 0:last], scalar=alpha, in1=fin[:, 1, 0:last], op0=ALU.mult, op1=ALU.mult
        )
        nc.vector.scalar_tensor_tensor(
            out=fin[:, 3, 0:last], in0=fin[:, 2, 0:last], scalar=beta, in1=fin[:, 0, 0:last], op0=ALU.add, op1=ALU.mult
        )
        nc.scalar.activation(
            out=last_square, in_=ssq[:, TILES - 1, 1:2], func=ACT.Square, bias=ssq[:, TILES - 1, 0:1]
        )
        nc.vector.tensor_scalar(
            out=fin[:, 3, last:], in0=last_square, scalar1=last_scale, scalar2=last_shift, op0=ALU.mult, op1=ALU.add
        )
        nc.sync.dma_start(out=out_v, in_=fin[:, 3, :])
